import numpy as np
import ml_dtypes


def mxq(x, axis, fmt="e4m3"):
    dtype, down = {"e4m3": (ml_dtypes.float8_e4m3fn, 7), "e5m2": (ml_dtypes.float8_e5m2, 14)}[fmt]
    v = np.moveaxis(np.asarray(x, np.float32).astype(ml_dtypes.bfloat16).astype(np.float64), axis, -1)
    blocks = v.reshape(v.shape[:-1] + (-1, 32))
    amax = np.abs(blocks).max(-1, keepdims=True)
    byte = np.maximum(np.where(amax > 0, np.frexp(amax)[1] - 1 + 127, 0) - down, 1)
    scale = np.exp2(byte - 127.0)
    codes = (blocks / scale).astype(np.float32).astype(dtype).astype(np.float64)
    return np.moveaxis((codes * scale).reshape(v.shape), -1, axis)


WIDE = False


def mx_kscale(k):
    if not WIDE:
        return np.ones(k)
    levels = np.array([10, -10, 5, -5, 0])
    a = np.random.permutation(np.resize(levels, k // 512 * 4)).reshape(k // 512, 4)
    idx = np.arange(k)
    return np.exp2(a[idx // 512, idx % 128 // 32])


BF16 = ml_dtypes.bfloat16


def bf(x):
    return np.asarray(x, np.float32).astype(BF16)


def f64(x):
    return np.asarray(x).astype(np.float64)


N, NR, F, C, R = 128, 1024, 1024, 128, 8
EPS = 1e-8


def encode_amplitude(v):
    return v / (np.linalg.norm(v, axis=1, keepdims=True) + EPS)


def setup_inputs():
    s = mx_kscale(F)
    basis = np.random.standard_normal((R, F)) / np.sqrt(R)
    x = np.random.standard_normal((N, R)) @ basis + 0.5 * np.random.standard_normal((N, F))
    x_ref = np.random.standard_normal((NR, R)) @ basis + 0.5 * np.random.standard_normal((NR, F))
    c = 2.0 ** np.round(np.log2(np.mean(s ** 2) * np.mean(s ** -2.0)))
    return {"x": bf(x * s), "x_ref": bf(x_ref / s),
            "mean_": bf(np.random.standard_normal(F) * 0.5 * np.minimum(s, 1.0 / s)),
            "components_": bf(np.random.standard_normal((C, NR)) * 8.0 / np.sqrt(NR) * c)}


def reference(x, x_ref, mean_, components_):
    xs = f64(x) - f64(mean_)
    xr = f64(x_ref) - f64(mean_)
    s1 = encode_amplitude(xs)
    s2 = encode_amplitude(xr)
    ov = mxq(s1, 1, "e4m3") @ mxq(s2, 1, "e4m3").T
    K = ov * ov
    return mxq(K, 1, "e4m3") @ mxq(f64(components_), 1, "e4m3").T

@@ -1,0 +1,185 @@
+from contextlib import ExitStack
+
+import concourse.mybir as mybir
+from concourse.masks import make_identity
+
+BF16 = mybir.dt.bfloat16
+F32 = mybir.dt.float32
+U32 = mybir.dt.uint32
+U8 = mybir.dt.uint8
+FP8X4 = mybir.dt.float8_e4m3fn_x4
+ACT = mybir.ActivationFunctionType
+ALU = mybir.AluOpType
+
+P = 128
+PACK = 4
+K_PASS = P * PACK
+N, NR, F, C = 128, 1024, 1024, 128
+EPS = 1e-8
+F_PASSES = F // K_PASS
+R_PASSES = NR // K_PASS
+ROW_TILES = 1 + NR // P
+FLOPS = 2 * N * NR * F + 2 * N * C * NR
+
+
+def tile_quantumkernelpca_s_kernel(tc, x, x_ref, mean_, components_, out):
+    nc = tc.nc
+    with ExitStack() as ctx:
+        keep = ctx.enter_context(tc.tile_pool(name="keep", bufs=1))
+        work = ctx.enter_context(tc.tile_pool(name="work", bufs=3))
+        flip_banks = ctx.enter_context(tc.psum_pool(name="flip_banks", bufs=3))
+        ov_banks = ctx.enter_context(tc.psum_pool(name="ov_banks", bufs=2))
+        last_banks = ctx.enter_context(tc.psum_pool(name="last_banks", bufs=1))
+
+        x_sb = keep.tile([P, F], BF16)
+        mean_bc = keep.tile([P, F], BF16)
+        ref_sb = keep.tile([P, R_PASSES, PACK, F], BF16)
+        comp_sb = keep.tile([P, NR], BF16)
+        nc.sync.dma_start(out=x_sb[:], in_=x)
+        nc.scalar.dma_start(out=mean_bc[:], in_=mean_.partition_broadcast(P))
+        ref_rows = x_ref.rearrange("(g p t) f -> g p t f", g=R_PASSES, p=P, t=PACK)
+        for g in range(R_PASSES):
+            nc.sync.dma_start(out=ref_sb[:, g, :, :], in_=ref_rows[g])
+        nc.scalar.dma_start(out=comp_sb[:], in_=components_)
+
+        ident_bf16 = keep.tile([P, P], BF16)
+        make_identity(nc, ident_bf16[:])
+        ident_f32 = keep.tile([P, P], F32)
+        make_identity(nc, ident_f32[:])
+
+        one = keep.tile([P, 1], F32)
+        nc.vector.memset(one[:], 1.0)
+        one_root = keep.tile([P, 1], F32)
+        nc.scalar.activation(out=one_root[:], in_=one[:], func=ACT.Sqrt)
+
+        norm_sq = keep.tile([P, ROW_TILES], F32)
+        norm = keep.tile([P, ROW_TILES], F32)
+        norm_eps = keep.tile([P, ROW_TILES], F32)
+        inv_norm = keep.tile([P, ROW_TILES], F32)
+
+        state_codes = keep.tile([P, ROW_TILES, F_PASSES, P], U32, align_bytes=64)
+        state_scales = keep.tile([P, ROW_TILES, F_PASSES, P], U8, align_bytes=64)
+        comp_codes = keep.tile([P, R_PASSES, C], U32, align_bytes=64)
+        comp_scales = keep.tile([P, R_PASSES, C], U8, align_bytes=64)
+        kern_codes = keep.tile([P, R_PASSES, N], U32, align_bytes=64)
+        kern_scales = keep.tile([P, R_PASSES, N], U8, align_bytes=64)
+
+        out_acc = last_banks.tile([N, C], F32)
+
+        centred = {}
+        flipped = {}
+        packed = {}
+        overlap = {}
+
+        def rows_of(j):
+            if j == 0:
+                return x_sb[:]
+            g, t = divmod(j - 1, PACK)
+            return ref_sb[:, g, t, :]
+
+        def measure(j):
+            xs = work.tile([P, F], F32, name="xs")
+            centred[j] = xs
+            nc.vector.tensor_tensor(out=xs[:], in0=rows_of(j), in1=mean_bc[:], op=ALU.subtract)
+            squares = work.tile([P, F], BF16, name="squares")
+            nc.scalar.activation(
+                out=squares[:], in_=xs[:], func=ACT.Square, accum_out=norm_sq[:, j : j + 1]
+            )
+            nc.scalar.activation(out=norm[:, j : j + 1], in_=norm_sq[:, j : j + 1], func=ACT.Sqrt)
+
+        def normalise_and_flip(j):
+            nc.vector.tensor_scalar_add(
+                out=norm_eps[:, j : j + 1], in0=norm[:, j : j + 1], scalar1=EPS
+            )
+            nc.vector.reciprocal(out=inv_norm[:, j : j + 1], in_=norm_eps[:, j : j + 1])
+            state = work.tile([P, F], BF16, name="state")
+            nc.vector.tensor_scalar_mul(
+                out=state[:], in0=centred[j][:], scalar1=inv_norm[:, j : j + 1]
+            )
+            flip = flip_banks.tile([P, F // P, P], BF16, name="flip")
+            flipped[j] = flip
+            for b in range(F // P):
+                nc.tensor.transpose(flip[:, b, :], state[:, b * P : (b + 1) * P], ident_bf16[:])
+
+        def regroup(j):
+            grouped = work.tile([P, F_PASSES, P, PACK], BF16, name="grouped", align_bytes=64)
+            packed[j] = grouped
+            nc.scalar.copy(
+                out=grouped[:], in_=flipped[j][:].rearrange("p (c t) r -> p c r t", t=PACK)
+            )
+
+        def quantise_state(j):
+            nc.vector.quantize_mx(
+                out=state_codes[:, j, :, :].rearrange("p c r -> p (c r)").bitcast(FP8X4),
+                scales=state_scales[:, j, :, :].rearrange("p c r -> p (c r)"),
+                in_=packed[j][:].rearrange("p c r t -> p (c r t)"),
+            )
+
+        def overlaps(j):
+            g, t = divmod(j - 1, PACK)
+            if t == 0:
+                overlap[g] = ov_banks.tile([P, PACK, N], F32, name="ov")
+            for c in range(F_PASSES):
+                nc.tensor.matmul_mx(
+                    out=overlap[g][:, t, :],
+                    lhsT=state_codes[:, j, c, :].bitcast(FP8X4),
+                    lhsT_scale=state_scales[:, j, c, :],
+                    rhs=state_codes[:, 0, c, :].bitcast(FP8X4),
+                    rhs_scale=state_scales[:, 0, c, :],
+                    start=(c == 0),
+                    stop=(c == F_PASSES - 1),
+                )
+
+        def project(g):
+            words = comp_sb[:].bitcast(F32).rearrange("c (g p u) -> c g u p", g=R_PASSES, u=2)
+            comp_flip = last_banks.tile([P, 2, C], F32, name="comp_flip")
+            for u in range(2):
+                nc.tensor.transpose(comp_flip[:, u, :], words[:, g, u, :], ident_f32[:])
+            kern_grouped = work.tile([P, N, PACK], BF16, name="kern_grouped", align_bytes=64)
+            nc.scalar.activation(
+                out=kern_grouped[:], in_=overlap[g][:].rearrange("p t n -> p n t"), func=ACT.Square
+            )
+            comp_grouped = work.tile([P, C, PACK], BF16, name="comp_grouped", align_bytes=64)
+            nc.vector.tensor_copy(
+                out=comp_grouped[:].rearrange("p c t -> p (c t)").bitcast(F32).rearrange(
+                    "p (c u) -> p c u", u=2
+                ),
+                in_=comp_flip[:].rearrange("p u c -> p c u"),
+            )
+            nc.vector.quantize_mx(
+                out=comp_codes[:, g, :].bitcast(FP8X4),
+                scales=comp_scales[:, g, :],
+                in_=comp_grouped[:].rearrange("p c t -> p (c t)"),
+            )
+            nc.vector.quantize_mx(
+                out=kern_codes[:, g, :].bitcast(FP8X4),
+                scales=kern_scales[:, g, :],
+                in_=kern_grouped[:].rearrange("p n t -> p (n t)"),
+            )
+            nc.tensor.matmul_mx(
+                out=out_acc[:],
+                lhsT=kern_codes[:, g, :].bitcast(FP8X4),
+                lhsT_scale=kern_scales[:, g, :],
+                rhs=comp_codes[:, g, :].bitcast(FP8X4),
+                rhs_scale=comp_scales[:, g, :],
+                start=(g == 0),
+                stop=(g == R_PASSES - 1),
+            )
+
+        for k in range(ROW_TILES + 3):
+            if 0 <= k - 2 < ROW_TILES:
+                regroup(k - 2)
+            if k - 3 >= 1 and (k - 3 - 1) % PACK == PACK - 1:
+                project((k - 3 - 1) // PACK)
+            if k < ROW_TILES:
+                measure(k)
+            if 0 <= k - 1 < ROW_TILES:
+                normalise_and_flip(k - 1)
+            if 0 <= k - 2 < ROW_TILES:
+                quantise_state(k - 2)
+            if 1 <= k - 2 < ROW_TILES:
+                overlaps(k - 2)
+
+        result = keep.tile([N, C], F32)
+        nc.vector.tensor_copy(out=result[:], in_=out_acc[:])
+        nc.sync.dma_start(out=out, in_=result[:])

@@ -19,7 +19,14 @@ EPS = 1e-8
 F_PASSES = F // K_PASS
 R_PASSES = NR // K_PASS
 ROW_TILES = 1 + NR // P
+GROUPS = ((0, 1 + PACK), (1 + PACK, ROW_TILES))
 FLOPS = 2 * N * NR * F + 2 * N * C * NR
+
+
+def pass_ending_at(j):
+    if j >= 1 and j < ROW_TILES and (j - 1) % PACK == PACK - 1:
+        return (j - 1) // PACK
+    return None
 
 
 def tile_quantumkernelpca_s_kernel(tc, x, x_ref, mean_, components_, out):
@@ -27,31 +34,34 @@ def tile_quantumkernelpca_s_kernel(tc, x, x_ref, mean_, components_, out):
     with ExitStack() as ctx:
         keep = ctx.enter_context(tc.tile_pool(name="keep", bufs=1))
         work = ctx.enter_context(tc.tile_pool(name="work", bufs=3))
-        flip_banks = ctx.enter_context(tc.psum_pool(name="flip_banks", bufs=3))
+        flip_banks = ctx.enter_context(tc.psum_pool(name="flip_banks", bufs=4))
         ov_banks = ctx.enter_context(tc.psum_pool(name="ov_banks", bufs=2))
         last_banks = ctx.enter_context(tc.psum_pool(name="last_banks", bufs=1))
+        ctx.enter_context(tc.manual_schedule())
 
+        comp_sb = keep.tile([P, NR], BF16)
         x_sb = keep.tile([P, F], BF16)
         mean_bc = keep.tile([P, F], BF16)
         ref_sb = keep.tile([P, R_PASSES, PACK, F], BF16)
-        comp_sb = keep.tile([P, NR], BF16)
-        nc.sync.dma_start(out=x_sb[:], in_=x)
         nc.scalar.dma_start(out=mean_bc[:], in_=mean_.partition_broadcast(P))
+        nc.sync.dma_start(out=comp_sb[:], in_=components_)
+        nc.sync.dma_start(out=x_sb[:], in_=x)
         ref_rows = x_ref.rearrange("(g p t) f -> g p t f", g=R_PASSES, p=P, t=PACK)
         for g in range(R_PASSES):
-            nc.sync.dma_start(out=ref_sb[:, g, :, :], in_=ref_rows[g])
-        nc.scalar.dma_start(out=comp_sb[:], in_=components_)
+            for t in range(0, PACK, 2):
+                nc.sync.dma_start(out=ref_sb[:, g, t : t + 2, :], in_=ref_rows[g, :, t : t + 2, :])
 
-        ident_bf16 = keep.tile([P, P], BF16)
-        make_identity(nc, ident_bf16[:])
         ident_f32 = keep.tile([P, P], F32)
         make_identity(nc, ident_f32[:])
+        ident_bf16 = keep.tile([P, P], BF16)
+        make_identity(nc, ident_bf16[:])
 
         one = keep.tile([P, 1], F32)
         nc.vector.memset(one[:], 1.0)
         one_root = keep.tile([P, 1], F32)
         nc.scalar.activation(out=one_root[:], in_=one[:], func=ACT.Sqrt)
 
+        centred = keep.tile([P, ROW_TILES, F], F32)
         norm_sq = keep.tile([P, ROW_TILES], F32)
         norm = keep.tile([P, ROW_TILES], F32)
         norm_eps = keep.tile([P, ROW_TILES], F32)
@@ -66,10 +76,27 @@ def tile_quantumkernelpca_s_kernel(tc, x, x_ref, mean_, components_, out):
 
         out_acc = last_banks.tile([N, C], F32)
 
-        centred = {}
         flipped = {}
         packed = {}
         overlap = {}
+        kernel = {}
+
+        def quantise_components():
+            words = comp_sb[:].bitcast(F32).rearrange("c (g p u) -> c g u p", g=R_PASSES, u=2)
+            comp_flip = last_banks.tile([P, R_PASSES, 2, C], F32)
+            for g in range(R_PASSES):
+                for u in range(2):
+                    nc.tensor.transpose(comp_flip[:, g, u, :], words[:, g, u, :], ident_f32[:])
+            comp_grouped = keep.tile([P, R_PASSES * C * PACK], BF16, align_bytes=64)
+            nc.scalar.copy(
+                out=comp_grouped[:].bitcast(F32).rearrange("p (g c u) -> p g c u", g=R_PASSES, u=2),
+                in_=comp_flip[:].rearrange("p g u c -> p g c u"),
+            )
+            nc.vector.quantize_mx(
+                out=comp_codes[:].rearrange("p g c -> p (g c)").bitcast(FP8X4),
+                scales=comp_scales[:].rearrange("p g c -> p (g c)"),
+                in_=comp_grouped[:],
+            )
 
         def rows_of(j):
             if j == 0:
@@ -78,23 +105,26 @@ def tile_quantumkernelpca_s_kernel(tc, x, x_ref, mean_, components_, out):
             return ref_sb[:, g, t, :]
 
         def measure(j):
-            xs = work.tile([P, F], F32, name="xs")
-            centred[j] = xs
-            nc.vector.tensor_tensor(out=xs[:], in0=rows_of(j), in1=mean_bc[:], op=ALU.subtract)
+            nc.vector.tensor_tensor(
+                out=centred[:, j, :], in0=rows_of(j), in1=mean_bc[:], op=ALU.subtract
+            )
             squares = work.tile([P, F], BF16, name="squares")
             nc.scalar.activation(
-                out=squares[:], in_=xs[:], func=ACT.Square, accum_out=norm_sq[:, j : j + 1]
+                out=squares[:], in_=centred[:, j, :], func=ACT.Square,
+                accum_out=norm_sq[:, j : j + 1],
             )
-            nc.scalar.activation(out=norm[:, j : j + 1], in_=norm_sq[:, j : j + 1], func=ACT.Sqrt)
+
+        def roots(lo, hi):
+            nc.scalar.activation(out=norm[:, lo:hi], in_=norm_sq[:, lo:hi], func=ACT.Sqrt)
+
+        def invert(lo, hi):
+            nc.vector.tensor_scalar_add(out=norm_eps[:, lo:hi], in0=norm[:, lo:hi], scalar1=EPS)
+            nc.vector.reciprocal(out=inv_norm[:, lo:hi], in_=norm_eps[:, lo:hi])
 
         def normalise_and_flip(j):
-            nc.vector.tensor_scalar_add(
-                out=norm_eps[:, j : j + 1], in0=norm[:, j : j + 1], scalar1=EPS
-            )
-            nc.vector.reciprocal(out=inv_norm[:, j : j + 1], in_=norm_eps[:, j : j + 1])
             state = work.tile([P, F], BF16, name="state")
             nc.vector.tensor_scalar_mul(
-                out=state[:], in0=centred[j][:], scalar1=inv_norm[:, j : j + 1]
+                out=state[:], in0=centred[:, j, :], scalar1=inv_norm[:, j : j + 1]
             )
             flip = flip_banks.tile([P, F // P, P], BF16, name="flip")
             flipped[j] = flip
@@ -104,9 +134,11 @@ def tile_quantumkernelpca_s_kernel(tc, x, x_ref, mean_, components_, out):
         def regroup(j):
             grouped = work.tile([P, F_PASSES, P, PACK], BF16, name="grouped", align_bytes=64)
             packed[j] = grouped
-            nc.scalar.copy(
-                out=grouped[:], in_=flipped[j][:].rearrange("p (c t) r -> p c r t", t=PACK)
-            )
+            by_words = flipped[j][:].rearrange("p (c t) r -> p c r t", t=PACK)
+            if j == 0 or j == ROW_TILES - 1:
+                nc.vector.tensor_copy(out=grouped[:], in_=by_words)
+            else:
+                nc.scalar.copy(out=grouped[:], in_=by_words)
 
         def quantise_state(j):
             nc.vector.quantize_mx(
@@ -130,31 +162,18 @@ def tile_quantumkernelpca_s_kernel(tc, x, x_ref, mean_, components_, out):
                     stop=(c == F_PASSES - 1),
                 )
 
-        def project(g):
-            words = comp_sb[:].bitcast(F32).rearrange("c (g p u) -> c g u p", g=R_PASSES, u=2)
-            comp_flip = last_banks.tile([P, 2, C], F32, name="comp_flip")
-            for u in range(2):
-                nc.tensor.transpose(comp_flip[:, u, :], words[:, g, u, :], ident_f32[:])
+        def square_overlaps(g):
             kern_grouped = work.tile([P, N, PACK], BF16, name="kern_grouped", align_bytes=64)
+            kernel[g] = kern_grouped
             nc.scalar.activation(
                 out=kern_grouped[:], in_=overlap[g][:].rearrange("p t n -> p n t"), func=ACT.Square
             )
-            comp_grouped = work.tile([P, C, PACK], BF16, name="comp_grouped", align_bytes=64)
-            nc.vector.tensor_copy(
-                out=comp_grouped[:].rearrange("p c t -> p (c t)").bitcast(F32).rearrange(
-                    "p (c u) -> p c u", u=2
-                ),
-                in_=comp_flip[:].rearrange("p u c -> p c u"),
-            )
-            nc.vector.quantize_mx(
-                out=comp_codes[:, g, :].bitcast(FP8X4),
-                scales=comp_scales[:, g, :],
-                in_=comp_grouped[:].rearrange("p c t -> p (c t)"),
-            )
+
+        def project(g):
             nc.vector.quantize_mx(
                 out=kern_codes[:, g, :].bitcast(FP8X4),
                 scales=kern_scales[:, g, :],
-                in_=kern_grouped[:].rearrange("p n t -> p (n t)"),
+                in_=kernel[g][:].rearrange("p n t -> p (n t)"),
             )
             nc.tensor.matmul_mx(
                 out=out_acc[:],
@@ -166,19 +185,29 @@ def tile_quantumkernelpca_s_kernel(tc, x, x_ref, mean_, components_, out):
                 stop=(g == R_PASSES - 1),
             )
 
-        for k in range(ROW_TILES + 3):
+        quantise_components()
+
+        for lo, hi in GROUPS:
+            for j in range(lo, hi):
+                measure(j)
+            roots(lo, hi)
+
+        for k in range(ROW_TILES + 5):
+            if pass_ending_at(k - 5) is not None:
+                project(pass_ending_at(k - 5))
+            for lo, hi in GROUPS:
+                if k == lo:
+                    invert(lo, hi)
+            if k < ROW_TILES:
+                normalise_and_flip(k)
             if 0 <= k - 2 < ROW_TILES:
                 regroup(k - 2)
-            if k - 3 >= 1 and (k - 3 - 1) % PACK == PACK - 1:
-                project((k - 3 - 1) // PACK)
-            if k < ROW_TILES:
-                measure(k)
-            if 0 <= k - 1 < ROW_TILES:
-                normalise_and_flip(k - 1)
-            if 0 <= k - 2 < ROW_TILES:
-                quantise_state(k - 2)
-            if 1 <= k - 2 < ROW_TILES:
-                overlaps(k - 2)
+            if 0 <= k - 3 < ROW_TILES:
+                quantise_state(k - 3)
+            if 1 <= k - 3 < ROW_TILES:
+                overlaps(k - 3)
+            if pass_ending_at(k - 4) is not None:
+                square_overlaps(pass_ending_at(k - 4))
 
         result = keep.tile([N, C], F32)
         nc.vector.tensor_copy(out=result[:], in_=out_acc[:])

@@ -19,8 +19,12 @@ EPS = 1e-8
 F_PASSES = F // K_PASS
 R_PASSES = NR // K_PASS
 ROW_TILES = 1 + NR // P
-GROUPS = ((0, 1 + PACK), (1 + PACK, ROW_TILES))
+VECTOR_COPIES_EVERY = 4
 FLOPS = 2 * N * NR * F + 2 * N * C * NR
+
+
+def is_row_tile(j):
+    return 0 <= j < ROW_TILES
 
 
 def pass_ending_at(j):
@@ -61,7 +65,6 @@ def tile_quantumkernelpca_s_kernel(tc, x, x_ref, mean_, components_, out):
         one_root = keep.tile([P, 1], F32)
         nc.scalar.activation(out=one_root[:], in_=one[:], func=ACT.Sqrt)
 
-        centred = keep.tile([P, ROW_TILES, F], F32)
         norm_sq = keep.tile([P, ROW_TILES], F32)
         norm = keep.tile([P, ROW_TILES], F32)
         norm_eps = keep.tile([P, ROW_TILES], F32)
@@ -76,6 +79,8 @@ def tile_quantumkernelpca_s_kernel(tc, x, x_ref, mean_, components_, out):
 
         out_acc = last_banks.tile([N, C], F32)
 
+        centred = {}
+        states = {}
         flipped = {}
         packed = {}
         overlap = {}
@@ -104,38 +109,40 @@ def tile_quantumkernelpca_s_kernel(tc, x, x_ref, mean_, components_, out):
             g, t = divmod(j - 1, PACK)
             return ref_sb[:, g, t, :]
 
-        def measure(j):
-            nc.vector.tensor_tensor(
-                out=centred[:, j, :], in0=rows_of(j), in1=mean_bc[:], op=ALU.subtract
-            )
+        def subtract_mean(j):
+            xs = work.tile([P, F], F32, name="xs")
+            centred[j] = xs
+            nc.vector.tensor_tensor(out=xs[:], in0=rows_of(j), in1=mean_bc[:], op=ALU.subtract)
+
+        def row_norms(j):
             squares = work.tile([P, F], BF16, name="squares")
             nc.scalar.activation(
-                out=squares[:], in_=centred[:, j, :], func=ACT.Square,
-                accum_out=norm_sq[:, j : j + 1],
+                out=squares[:], in_=centred[j][:], func=ACT.Square, accum_out=norm_sq[:, j : j + 1]
             )
+            nc.scalar.activation(out=norm[:, j : j + 1], in_=norm_sq[:, j : j + 1], func=ACT.Sqrt)
 
-        def roots(lo, hi):
-            nc.scalar.activation(out=norm[:, lo:hi], in_=norm_sq[:, lo:hi], func=ACT.Sqrt)
-
-        def invert(lo, hi):
-            nc.vector.tensor_scalar_add(out=norm_eps[:, lo:hi], in0=norm[:, lo:hi], scalar1=EPS)
-            nc.vector.reciprocal(out=inv_norm[:, lo:hi], in_=norm_eps[:, lo:hi])
-
-        def normalise_and_flip(j):
+        def normalise(j):
+            nc.vector.tensor_scalar_add(
+                out=norm_eps[:, j : j + 1], in0=norm[:, j : j + 1], scalar1=EPS
+            )
+            nc.vector.reciprocal(out=inv_norm[:, j : j + 1], in_=norm_eps[:, j : j + 1])
             state = work.tile([P, F], BF16, name="state")
+            states[j] = state
             nc.vector.tensor_scalar_mul(
-                out=state[:], in0=centred[:, j, :], scalar1=inv_norm[:, j : j + 1]
+                out=state[:], in0=centred[j][:], scalar1=inv_norm[:, j : j + 1]
             )
-            flip = flip_banks.tile([P, F // P, P], BF16, name="flip")
-            flipped[j] = flip
+
+        def flip(j):
+            bank = flip_banks.tile([P, F // P, P], BF16, name="bank")
+            flipped[j] = bank
             for b in range(F // P):
-                nc.tensor.transpose(flip[:, b, :], state[:, b * P : (b + 1) * P], ident_bf16[:])
+                nc.tensor.transpose(bank[:, b, :], states[j][:, b * P : (b + 1) * P], ident_bf16[:])
 
         def regroup(j):
             grouped = work.tile([P, F_PASSES, P, PACK], BF16, name="grouped", align_bytes=64)
             packed[j] = grouped
             by_words = flipped[j][:].rearrange("p (c t) r -> p c r t", t=PACK)
-            if j == 0 or j == ROW_TILES - 1:
+            if j % VECTOR_COPIES_EVERY == VECTOR_COPIES_EVERY - 1:
                 nc.vector.tensor_copy(out=grouped[:], in_=by_words)
             else:
                 nc.scalar.copy(out=grouped[:], in_=by_words)
@@ -187,27 +194,25 @@ def tile_quantumkernelpca_s_kernel(tc, x, x_ref, mean_, components_, out):
 
         quantise_components()
 
-        for lo, hi in GROUPS:
-            for j in range(lo, hi):
-                measure(j)
-            roots(lo, hi)
-
-        for k in range(ROW_TILES + 5):
-            if pass_ending_at(k - 5) is not None:
-                project(pass_ending_at(k - 5))
-            for lo, hi in GROUPS:
-                if k == lo:
-                    invert(lo, hi)
-            if k < ROW_TILES:
-                normalise_and_flip(k)
-            if 0 <= k - 2 < ROW_TILES:
+        for k in range(-1, ROW_TILES + 5):
+            if is_row_tile(k + 1):
+                subtract_mean(k + 1)
+            if is_row_tile(k):
+                row_norms(k)
+            if is_row_tile(k - 1):
+                flip(k - 1)
+            if is_row_tile(k - 2):
                 regroup(k - 2)
-            if 0 <= k - 3 < ROW_TILES:
+            if is_row_tile(k - 3):
                 quantise_state(k - 3)
-            if 1 <= k - 3 < ROW_TILES:
+            if is_row_tile(k - 3) and k - 3 > 0:
                 overlaps(k - 3)
             if pass_ending_at(k - 4) is not None:
                 square_overlaps(pass_ending_at(k - 4))
+            if pass_ending_at(k - 5) is not None:
+                project(pass_ending_at(k - 5))
+            if is_row_tile(k):
+                normalise(k)
 
         result = keep.tile([N, C], F32)
         nc.vector.tensor_copy(out=result[:], in_=out_acc[:])

@@ -19,12 +19,8 @@ EPS = 1e-8
 F_PASSES = F // K_PASS
 R_PASSES = NR // K_PASS
 ROW_TILES = 1 + NR // P
-VECTOR_COPIES_EVERY = 4
+GROUPS = ((0, 1 + PACK), (1 + PACK, ROW_TILES))
 FLOPS = 2 * N * NR * F + 2 * N * C * NR
-
-
-def is_row_tile(j):
-    return 0 <= j < ROW_TILES
 
 
 def pass_ending_at(j):
@@ -48,12 +44,12 @@ def tile_quantumkernelpca_s_kernel(tc, x, x_ref, mean_, components_, out):
         mean_bc = keep.tile([P, F], BF16)
         ref_sb = keep.tile([P, R_PASSES, PACK, F], BF16)
         nc.scalar.dma_start(out=mean_bc[:], in_=mean_.partition_broadcast(P))
-        nc.sync.dma_start(out=comp_sb[:], in_=components_)
         nc.sync.dma_start(out=x_sb[:], in_=x)
         ref_rows = x_ref.rearrange("(g p t) f -> g p t f", g=R_PASSES, p=P, t=PACK)
         for g in range(R_PASSES):
             for t in range(0, PACK, 2):
                 nc.sync.dma_start(out=ref_sb[:, g, t : t + 2, :], in_=ref_rows[g, :, t : t + 2, :])
+        nc.sync.dma_start(out=comp_sb[:], in_=components_)
 
         ident_f32 = keep.tile([P, P], F32)
         make_identity(nc, ident_f32[:])
@@ -65,6 +61,7 @@ def tile_quantumkernelpca_s_kernel(tc, x, x_ref, mean_, components_, out):
         one_root = keep.tile([P, 1], F32)
         nc.scalar.activation(out=one_root[:], in_=one[:], func=ACT.Sqrt)
 
+        centred = keep.tile([P, ROW_TILES, F], F32)
         norm_sq = keep.tile([P, ROW_TILES], F32)
         norm = keep.tile([P, ROW_TILES], F32)
         norm_eps = keep.tile([P, ROW_TILES], F32)
@@ -79,28 +76,26 @@ def tile_quantumkernelpca_s_kernel(tc, x, x_ref, mean_, components_, out):
 
         out_acc = last_banks.tile([N, C], F32)
 
-        centred = {}
-        states = {}
         flipped = {}
         packed = {}
         overlap = {}
         kernel = {}
 
-        def quantise_components():
+        comp_flip = last_banks.tile([P, R_PASSES, 2, C], F32)
+        comp_grouped = keep.tile([P, R_PASSES, C * PACK], BF16, align_bytes=64)
+
+        def flip_components():
             words = comp_sb[:].bitcast(F32).rearrange("c (g p u) -> c g u p", g=R_PASSES, u=2)
-            comp_flip = last_banks.tile([P, R_PASSES, 2, C], F32)
             for g in range(R_PASSES):
                 for u in range(2):
                     nc.tensor.transpose(comp_flip[:, g, u, :], words[:, g, u, :], ident_f32[:])
-            comp_grouped = keep.tile([P, R_PASSES * C * PACK], BF16, align_bytes=64)
+
+        def regroup_components():
             nc.scalar.copy(
-                out=comp_grouped[:].bitcast(F32).rearrange("p (g c u) -> p g c u", g=R_PASSES, u=2),
+                out=comp_grouped[:].rearrange("p g w -> p (g w)").bitcast(F32).rearrange(
+                    "p (g c u) -> p g c u", g=R_PASSES, u=2
+                ),
                 in_=comp_flip[:].rearrange("p g u c -> p g c u"),
-            )
-            nc.vector.quantize_mx(
-                out=comp_codes[:].rearrange("p g c -> p (g c)").bitcast(FP8X4),
-                scales=comp_scales[:].rearrange("p g c -> p (g c)"),
-                in_=comp_grouped[:],
             )
 
         def rows_of(j):
@@ -109,40 +104,38 @@ def tile_quantumkernelpca_s_kernel(tc, x, x_ref, mean_, components_, out):
             g, t = divmod(j - 1, PACK)
             return ref_sb[:, g, t, :]
 
-        def subtract_mean(j):
-            xs = work.tile([P, F], F32, name="xs")
-            centred[j] = xs
-            nc.vector.tensor_tensor(out=xs[:], in0=rows_of(j), in1=mean_bc[:], op=ALU.subtract)
-
-        def row_norms(j):
+        def measure(j):
+            nc.vector.tensor_tensor(
+                out=centred[:, j, :], in0=rows_of(j), in1=mean_bc[:], op=ALU.subtract
+            )
             squares = work.tile([P, F], BF16, name="squares")
             nc.scalar.activation(
-                out=squares[:], in_=centred[j][:], func=ACT.Square, accum_out=norm_sq[:, j : j + 1]
+                out=squares[:], in_=centred[:, j, :], func=ACT.Square,
+                accum_out=norm_sq[:, j : j + 1],
             )
-            nc.scalar.activation(out=norm[:, j : j + 1], in_=norm_sq[:, j : j + 1], func=ACT.Sqrt)
 
-        def normalise(j):
-            nc.vector.tensor_scalar_add(
-                out=norm_eps[:, j : j + 1], in0=norm[:, j : j + 1], scalar1=EPS
-            )
-            nc.vector.reciprocal(out=inv_norm[:, j : j + 1], in_=norm_eps[:, j : j + 1])
+        def roots(lo, hi):
+            nc.scalar.activation(out=norm[:, lo:hi], in_=norm_sq[:, lo:hi], func=ACT.Sqrt)
+
+        def invert(lo, hi):
+            nc.vector.tensor_scalar_add(out=norm_eps[:, lo:hi], in0=norm[:, lo:hi], scalar1=EPS)
+            nc.vector.reciprocal(out=inv_norm[:, lo:hi], in_=norm_eps[:, lo:hi])
+
+        def normalise_and_flip(j):
             state = work.tile([P, F], BF16, name="state")
-            states[j] = state
             nc.vector.tensor_scalar_mul(
-                out=state[:], in0=centred[j][:], scalar1=inv_norm[:, j : j + 1]
+                out=state[:], in0=centred[:, j, :], scalar1=inv_norm[:, j : j + 1]
             )
-
-        def flip(j):
-            bank = flip_banks.tile([P, F // P, P], BF16, name="bank")
-            flipped[j] = bank
+            flip = flip_banks.tile([P, F // P, P], BF16, name="flip")
+            flipped[j] = flip
             for b in range(F // P):
-                nc.tensor.transpose(bank[:, b, :], states[j][:, b * P : (b + 1) * P], ident_bf16[:])
+                nc.tensor.transpose(flip[:, b, :], state[:, b * P : (b + 1) * P], ident_bf16[:])
 
         def regroup(j):
             grouped = work.tile([P, F_PASSES, P, PACK], BF16, name="grouped", align_bytes=64)
             packed[j] = grouped
             by_words = flipped[j][:].rearrange("p (c t) r -> p c r t", t=PACK)
-            if j % VECTOR_COPIES_EVERY == VECTOR_COPIES_EVERY - 1:
+            if j == ROW_TILES - 1:
                 nc.vector.tensor_copy(out=grouped[:], in_=by_words)
             else:
                 nc.scalar.copy(out=grouped[:], in_=by_words)
@@ -154,20 +147,20 @@ def tile_quantumkernelpca_s_kernel(tc, x, x_ref, mean_, components_, out):
                 in_=packed[j][:].rearrange("p c r t -> p (c r t)"),
             )
 
-        def overlaps(j):
-            g, t = divmod(j - 1, PACK)
-            if t == 0:
-                overlap[g] = ov_banks.tile([P, PACK, N], F32, name="ov")
-            for c in range(F_PASSES):
-                nc.tensor.matmul_mx(
-                    out=overlap[g][:, t, :],
-                    lhsT=state_codes[:, j, c, :].bitcast(FP8X4),
-                    lhsT_scale=state_scales[:, j, c, :],
-                    rhs=state_codes[:, 0, c, :].bitcast(FP8X4),
-                    rhs_scale=state_scales[:, 0, c, :],
-                    start=(c == 0),
-                    stop=(c == F_PASSES - 1),
-                )
+        def overlaps(g):
+            overlap[g] = ov_banks.tile([P, PACK, N], F32, name="ov")
+            for t in range(PACK):
+                j = 1 + g * PACK + t
+                for c in range(F_PASSES):
+                    nc.tensor.matmul_mx(
+                        out=overlap[g][:, t, :],
+                        lhsT=state_codes[:, j, c, :].bitcast(FP8X4),
+                        lhsT_scale=state_scales[:, j, c, :],
+                        rhs=state_codes[:, 0, c, :].bitcast(FP8X4),
+                        rhs_scale=state_scales[:, 0, c, :],
+                        start=(c == 0),
+                        stop=(c == F_PASSES - 1),
+                    )
 
         def square_overlaps(g):
             kern_grouped = work.tile([P, N, PACK], BF16, name="kern_grouped", align_bytes=64)
@@ -177,6 +170,11 @@ def tile_quantumkernelpca_s_kernel(tc, x, x_ref, mean_, components_, out):
             )
 
         def project(g):
+            nc.vector.quantize_mx(
+                out=comp_codes[:, g, :].bitcast(FP8X4),
+                scales=comp_scales[:, g, :],
+                in_=comp_grouped[:, g, :],
+            )
             nc.vector.quantize_mx(
                 out=kern_codes[:, g, :].bitcast(FP8X4),
                 scales=kern_scales[:, g, :],
@@ -192,27 +190,30 @@ def tile_quantumkernelpca_s_kernel(tc, x, x_ref, mean_, components_, out):
                 stop=(g == R_PASSES - 1),
             )
 
-        quantise_components()
+        flip_components()
 
-        for k in range(-1, ROW_TILES + 5):
-            if is_row_tile(k + 1):
-                subtract_mean(k + 1)
-            if is_row_tile(k):
-                row_norms(k)
-            if is_row_tile(k - 1):
-                flip(k - 1)
-            if is_row_tile(k - 2):
+        for lo, hi in GROUPS:
+            for j in range(lo, hi):
+                measure(j)
+            roots(lo, hi)
+        regroup_components()
+
+        for k in range(ROW_TILES + 6):
+            for lo, hi in GROUPS:
+                if k == lo:
+                    invert(lo, hi)
+            if k < ROW_TILES:
+                normalise_and_flip(k)
+            if 0 <= k - 2 < ROW_TILES:
                 regroup(k - 2)
-            if is_row_tile(k - 3):
+            if 0 <= k - 3 < ROW_TILES:
                 quantise_state(k - 3)
-            if is_row_tile(k - 3) and k - 3 > 0:
-                overlaps(k - 3)
+            if pass_ending_at(k - 3) is not None:
+                overlaps(pass_ending_at(k - 3))
             if pass_ending_at(k - 4) is not None:
                 square_overlaps(pass_ending_at(k - 4))
-            if pass_ending_at(k - 5) is not None:
-                project(pass_ending_at(k - 5))
-            if is_row_tile(k):
-                normalise(k)
+            if pass_ending_at(k - 6) is not None:
+                project(pass_ending_at(k - 6))
 
         result = keep.tile([N, C], F32)
         nc.vector.tensor_copy(out=result[:], in_=out_acc[:])

@@ -98,6 +98,13 @@ def tile_quantumkernelpca_s_kernel(tc, x, x_ref, mean_, components_, out):
                 in_=comp_flip[:].rearrange("p g u c -> p g c u"),
             )
 
+        def quantise_components():
+            nc.vector.quantize_mx(
+                out=comp_codes[:].rearrange("p g c -> p (g c)").bitcast(FP8X4),
+                scales=comp_scales[:].rearrange("p g c -> p (g c)"),
+                in_=comp_grouped[:].rearrange("p g w -> p (g w)"),
+            )
+
         def rows_of(j):
             if j == 0:
                 return x_sb[:]
@@ -135,7 +142,7 @@ def tile_quantumkernelpca_s_kernel(tc, x, x_ref, mean_, components_, out):
             grouped = work.tile([P, F_PASSES, P, PACK], BF16, name="grouped", align_bytes=64)
             packed[j] = grouped
             by_words = flipped[j][:].rearrange("p (c t) r -> p c r t", t=PACK)
-            if j == ROW_TILES - 1:
+            if j == 0 or j == ROW_TILES - 1:
                 nc.vector.tensor_copy(out=grouped[:], in_=by_words)
             else:
                 nc.scalar.copy(out=grouped[:], in_=by_words)
@@ -171,11 +178,6 @@ def tile_quantumkernelpca_s_kernel(tc, x, x_ref, mean_, components_, out):
 
         def project(g):
             nc.vector.quantize_mx(
-                out=comp_codes[:, g, :].bitcast(FP8X4),
-                scales=comp_scales[:, g, :],
-                in_=comp_grouped[:, g, :],
-            )
-            nc.vector.quantize_mx(
                 out=kern_codes[:, g, :].bitcast(FP8X4),
                 scales=kern_scales[:, g, :],
                 in_=kernel[g][:].rearrange("p n t -> p (n t)"),
@@ -196,9 +198,8 @@ def tile_quantumkernelpca_s_kernel(tc, x, x_ref, mean_, components_, out):
             for j in range(lo, hi):
                 measure(j)
             roots(lo, hi)
-        regroup_components()
 
-        for k in range(ROW_TILES + 6):
+        for k in range(ROW_TILES + 4):
             for lo, hi in GROUPS:
                 if k == lo:
                     invert(lo, hi)
@@ -210,10 +211,13 @@ def tile_quantumkernelpca_s_kernel(tc, x, x_ref, mean_, components_, out):
                 quantise_state(k - 3)
             if pass_ending_at(k - 3) is not None:
                 overlaps(pass_ending_at(k - 3))
+            if k - 3 == ROW_TILES - 1:
+                regroup_components()
+                quantise_components()
             if pass_ending_at(k - 4) is not None:
                 square_overlaps(pass_ending_at(k - 4))
-            if pass_ending_at(k - 6) is not None:
-                project(pass_ending_at(k - 6))
+        for g in range(R_PASSES):
+            project(g)
 
         result = keep.tile([N, C], F32)
         nc.vector.tensor_copy(out=result[:], in_=out_acc[:])

@@ -133,19 +133,22 @@ def tile_quantumkernelpca_s_kernel(tc, x, x_ref, mean_, components_, out):
             nc.vector.tensor_scalar_mul(
                 out=state[:], in0=centred[:, j, :], scalar1=inv_norm[:, j : j + 1]
             )
-            flip = flip_banks.tile([P, F // P, P], BF16, name="flip")
-            flipped[j] = flip
-            for b in range(F // P):
-                nc.tensor.transpose(flip[:, b, :], state[:, b * P : (b + 1) * P], ident_bf16[:])
+            for c in range(F_PASSES):
+                bank = flip_banks.tile([P, PACK, P], BF16, name="bank")
+                flipped[j, c] = bank
+                for t in range(PACK):
+                    b = c * PACK + t
+                    nc.tensor.transpose(bank[:, t, :], state[:, b * P : (b + 1) * P], ident_bf16[:])
 
         def regroup(j):
             grouped = work.tile([P, F_PASSES, P, PACK], BF16, name="grouped", align_bytes=64)
             packed[j] = grouped
-            by_words = flipped[j][:].rearrange("p (c t) r -> p c r t", t=PACK)
-            if j == 0 or j == ROW_TILES - 1:
-                nc.vector.tensor_copy(out=grouped[:], in_=by_words)
-            else:
-                nc.scalar.copy(out=grouped[:], in_=by_words)
+            for c in range(F_PASSES):
+                by_words = flipped[j, c][:].rearrange("p t r -> p r t")
+                if j == 0 or j == ROW_TILES - 1:
+                    nc.vector.tensor_copy(out=grouped[:, c, :, :], in_=by_words)
+                else:
+                    nc.scalar.copy(out=grouped[:, c, :, :], in_=by_words)
 
         def quantise_state(j):
             nc.vector.quantize_mx(
@@ -199,23 +202,23 @@ def tile_quantumkernelpca_s_kernel(tc, x, x_ref, mean_, components_, out):
                 measure(j)
             roots(lo, hi)
 
-        for k in range(ROW_TILES + 4):
+        for k in range(ROW_TILES + 3):
             for lo, hi in GROUPS:
                 if k == lo:
                     invert(lo, hi)
             if k < ROW_TILES:
                 normalise_and_flip(k)
+            if 0 <= k - 1 < ROW_TILES:
+                regroup(k - 1)
             if 0 <= k - 2 < ROW_TILES:
-                regroup(k - 2)
-            if 0 <= k - 3 < ROW_TILES:
-                quantise_state(k - 3)
-            if pass_ending_at(k - 3) is not None:
-                overlaps(pass_ending_at(k - 3))
-            if k - 3 == ROW_TILES - 1:
+                quantise_state(k - 2)
+            if pass_ending_at(k - 2) is not None:
+                overlaps(pass_ending_at(k - 2))
+            if k - 2 == ROW_TILES - 1:
                 regroup_components()
                 quantise_components()
-            if pass_ending_at(k - 4) is not None:
-                square_overlaps(pass_ending_at(k - 4))
+            if pass_ending_at(k - 3) is not None:
+                square_overlaps(pass_ending_at(k - 3))
         for g in range(R_PASSES):
             project(g)
 

@@ -34,8 +34,8 @@ def tile_quantumkernelpca_s_kernel(tc, x, x_ref, mean_, components_, out):
     with ExitStack() as ctx:
         keep = ctx.enter_context(tc.tile_pool(name="keep", bufs=1))
         work = ctx.enter_context(tc.tile_pool(name="work", bufs=3))
-        flip_banks = ctx.enter_context(tc.psum_pool(name="flip_banks", bufs=4))
-        ov_banks = ctx.enter_context(tc.psum_pool(name="ov_banks", bufs=2))
+        flip_banks = ctx.enter_context(tc.psum_pool(name="flip_banks", bufs=6))
+        ov_banks = ctx.enter_context(tc.psum_pool(name="ov_banks", bufs=1))
         last_banks = ctx.enter_context(tc.psum_pool(name="last_banks", bufs=1))
         ctx.enter_context(tc.manual_schedule())
 
@@ -81,11 +81,12 @@ def tile_quantumkernelpca_s_kernel(tc, x, x_ref, mean_, components_, out):
         overlap = {}
         kernel = {}
 
-        comp_flip = last_banks.tile([P, R_PASSES, 2, C], F32)
         comp_grouped = keep.tile([P, R_PASSES, C * PACK], BF16, align_bytes=64)
 
         def flip_components():
             words = comp_sb[:].bitcast(F32).rearrange("c (g p u) -> c g u p", g=R_PASSES, u=2)
+            comp_flip = flip_banks.tile([P, R_PASSES, 2, C], F32, name="bank")
+            flipped["components"] = comp_flip
             for g in range(R_PASSES):
                 for u in range(2):
                     nc.tensor.transpose(comp_flip[:, g, u, :], words[:, g, u, :], ident_f32[:])
@@ -95,7 +96,7 @@ def tile_quantumkernelpca_s_kernel(tc, x, x_ref, mean_, components_, out):
                 out=comp_grouped[:].rearrange("p g w -> p (g w)").bitcast(F32).rearrange(
                     "p (g c u) -> p g c u", g=R_PASSES, u=2
                 ),
-                in_=comp_flip[:].rearrange("p g u c -> p g c u"),
+                in_=flipped["components"][:].rearrange("p g u c -> p g c u"),
             )
 
         def quantise_components():
@@ -195,30 +196,30 @@ def tile_quantumkernelpca_s_kernel(tc, x, x_ref, mean_, components_, out):
                 stop=(g == R_PASSES - 1),
             )
 
-        flip_components()
-
         for lo, hi in GROUPS:
             for j in range(lo, hi):
                 measure(j)
             roots(lo, hi)
 
-        for k in range(ROW_TILES + 3):
+        for k in range(ROW_TILES + 4):
             for lo, hi in GROUPS:
                 if k == lo:
                     invert(lo, hi)
             if k < ROW_TILES:
                 normalise_and_flip(k)
-            if 0 <= k - 1 < ROW_TILES:
-                regroup(k - 1)
             if 0 <= k - 2 < ROW_TILES:
-                quantise_state(k - 2)
-            if pass_ending_at(k - 2) is not None:
-                overlaps(pass_ending_at(k - 2))
-            if k - 2 == ROW_TILES - 1:
+                regroup(k - 2)
+            if k == ROW_TILES - 1:
+                flip_components()
+            if 0 <= k - 3 < ROW_TILES:
+                quantise_state(k - 3)
+            if pass_ending_at(k - 3) is not None:
+                overlaps(pass_ending_at(k - 3))
+            if k - 3 == ROW_TILES - 1:
                 regroup_components()
                 quantise_components()
-            if pass_ending_at(k - 3) is not None:
-                square_overlaps(pass_ending_at(k - 3))
+            if pass_ending_at(k - 4) is not None:
+                square_overlaps(pass_ending_at(k - 4))
         for g in range(R_PASSES):
             project(g)
 

@@ -201,7 +201,7 @@ def tile_quantumkernelpca_s_kernel(tc, x, x_ref, mean_, components_, out):
                 measure(j)
             roots(lo, hi)
 
-        for k in range(ROW_TILES + 4):
+        for k in range(ROW_TILES + 5):
             for lo, hi in GROUPS:
                 if k == lo:
                     invert(lo, hi)
@@ -209,17 +209,17 @@ def tile_quantumkernelpca_s_kernel(tc, x, x_ref, mean_, components_, out):
                 normalise_and_flip(k)
             if 0 <= k - 2 < ROW_TILES:
                 regroup(k - 2)
-            if k == ROW_TILES - 1:
-                flip_components()
             if 0 <= k - 3 < ROW_TILES:
                 quantise_state(k - 3)
-            if pass_ending_at(k - 3) is not None:
-                overlaps(pass_ending_at(k - 3))
+            if pass_ending_at(k - 4) is not None:
+                overlaps(pass_ending_at(k - 4))
+            if k == ROW_TILES - 1:
+                flip_components()
             if k - 3 == ROW_TILES - 1:
                 regroup_components()
                 quantise_components()
-            if pass_ending_at(k - 4) is not None:
-                square_overlaps(pass_ending_at(k - 4))
+            if pass_ending_at(k - 5) is not None:
+                square_overlaps(pass_ending_at(k - 5))
         for g in range(R_PASSES):
             project(g)
 

@@ -53,8 +53,6 @@ def tile_quantumkernelpca_s_kernel(tc, x, x_ref, mean_, components_, out):
 
         ident_f32 = keep.tile([P, P], F32)
         make_identity(nc, ident_f32[:])
-        ident_bf16 = keep.tile([P, P], BF16)
-        make_identity(nc, ident_bf16[:])
 
         one = keep.tile([P, 1], F32)
         nc.vector.memset(one[:], 1.0)
@@ -134,22 +132,24 @@ def tile_quantumkernelpca_s_kernel(tc, x, x_ref, mean_, components_, out):
             nc.vector.tensor_scalar_mul(
                 out=state[:], in0=centred[:, j, :], scalar1=inv_norm[:, j : j + 1]
             )
+            words = state[:].bitcast(F32).rearrange("r (c u p) -> r c u p", c=F_PASSES, u=2)
+            bank = flip_banks.tile([P, F_PASSES, 2, P], F32, name="bank")
+            flipped[j] = bank
             for c in range(F_PASSES):
-                bank = flip_banks.tile([P, PACK, P], BF16, name="bank")
-                flipped[j, c] = bank
-                for t in range(PACK):
-                    b = c * PACK + t
-                    nc.tensor.transpose(bank[:, t, :], state[:, b * P : (b + 1) * P], ident_bf16[:])
+                for u in range(2):
+                    nc.tensor.transpose(bank[:, c, u, :], words[:, c, u, :], ident_f32[:])
 
         def regroup(j):
             grouped = work.tile([P, F_PASSES, P, PACK], BF16, name="grouped", align_bytes=64)
             packed[j] = grouped
-            for c in range(F_PASSES):
-                by_words = flipped[j, c][:].rearrange("p t r -> p r t")
-                if j == 0 or j == ROW_TILES - 1:
-                    nc.vector.tensor_copy(out=grouped[:, c, :, :], in_=by_words)
-                else:
-                    nc.scalar.copy(out=grouped[:, c, :, :], in_=by_words)
+            pairs = grouped[:].rearrange("p c r t -> p (c r t)").bitcast(F32).rearrange(
+                "p (c r u) -> p c r u", c=F_PASSES, u=2
+            )
+            by_words = flipped[j][:].rearrange("p c u r -> p c r u")
+            if j == 0 or j == ROW_TILES - 1:
+                nc.vector.tensor_copy(out=pairs, in_=by_words)
+            else:
+                nc.scalar.copy(out=pairs, in_=by_words)
 
         def quantise_state(j):
             nc.vector.quantize_mx(

@@ -16,6 +16,7 @@ PACK = 4
 K_PASS = P * PACK
 N, NR, F, C = 128, 1024, 1024, 128
 EPS = 1e-8
+MEAN_WORDS = F // P // 2
 F_PASSES = F // K_PASS
 R_PASSES = NR // K_PASS
 ROW_TILES = 1 + NR // P
@@ -34,16 +35,17 @@ def tile_quantumkernelpca_s_kernel(tc, x, x_ref, mean_, components_, out):
     with ExitStack() as ctx:
         keep = ctx.enter_context(tc.tile_pool(name="keep", bufs=1))
         work = ctx.enter_context(tc.tile_pool(name="work", bufs=3))
-        flip_banks = ctx.enter_context(tc.psum_pool(name="flip_banks", bufs=6))
+        flip_banks = ctx.enter_context(tc.psum_pool(name="flip_banks", bufs=5))
         ov_banks = ctx.enter_context(tc.psum_pool(name="ov_banks", bufs=1))
+        mean_banks = ctx.enter_context(tc.psum_pool(name="mean_banks", bufs=1))
         last_banks = ctx.enter_context(tc.psum_pool(name="last_banks", bufs=1))
         ctx.enter_context(tc.manual_schedule())
 
         comp_sb = keep.tile([P, NR], BF16)
         x_sb = keep.tile([P, F], BF16)
-        mean_bc = keep.tile([P, F], BF16)
+        mean_sb = keep.tile([P, F // P], BF16)
         ref_sb = keep.tile([P, R_PASSES, PACK, F], BF16)
-        nc.scalar.dma_start(out=mean_bc[:], in_=mean_.partition_broadcast(P))
+        nc.scalar.dma_start(out=mean_sb[:], in_=mean_.rearrange("(p k) -> p k", p=P))
         nc.sync.dma_start(out=x_sb[:], in_=x)
         ref_rows = x_ref.rearrange("(g p t) f -> g p t f", g=R_PASSES, p=P, t=PACK)
         for g in range(R_PASSES):
@@ -53,6 +55,18 @@ def tile_quantumkernelpca_s_kernel(tc, x, x_ref, mean_, components_, out):
 
         ident_f32 = keep.tile([P, P], F32)
         make_identity(nc, ident_f32[:])
+
+        mean_bank = mean_banks.tile([P, MEAN_WORDS, P], F32)
+        for j in range(MEAN_WORDS):
+            nc.tensor.transpose(
+                mean_bank[:, j, :],
+                mean_sb[:].bitcast(F32)[:, j : j + 1].to_broadcast([P, P]),
+                ident_f32[:],
+            )
+        mean_bc = mean_bank[:].bitcast(BF16).rearrange("q j (p e) -> q p j e", e=2)
+
+        def by_mean_words(rows):
+            return rows.rearrange("q (p j e) -> q p j e", j=MEAN_WORDS, e=2)
 
         one = keep.tile([P, 1], F32)
         nc.vector.memset(one[:], 1.0)
@@ -112,7 +126,10 @@ def tile_quantumkernelpca_s_kernel(tc, x, x_ref, mean_, components_, out):
 
         def measure(j):
             nc.vector.tensor_tensor(
-                out=centred[:, j, :], in0=rows_of(j), in1=mean_bc[:], op=ALU.subtract
+                out=by_mean_words(centred[:, j, :]),
+                in0=by_mean_words(rows_of(j)),
+                in1=mean_bc,
+                op=ALU.subtract,
             )
             squares = work.tile([P, F], BF16, name="squares")
             nc.scalar.activation(

@@ -17,10 +17,11 @@ K_PASS = P * PACK
 N, NR, F, C = 128, 1024, 1024, 128
 EPS = 1e-8
 MEAN_WORDS = F // P // 2
+GPSIMD_TILES = (3, 6)
 F_PASSES = F // K_PASS
 R_PASSES = NR // K_PASS
 ROW_TILES = 1 + NR // P
-GROUPS = ((0, 1 + PACK), (1 + PACK, ROW_TILES))
+GROUPS = ((0, 4), (4, 7), (7, 9))
 FLOPS = 2 * N * NR * F + 2 * N * C * NR
 
 
@@ -34,10 +35,8 @@ def tile_quantumkernelpca_s_kernel(tc, x, x_ref, mean_, components_, out):
     nc = tc.nc
     with ExitStack() as ctx:
         keep = ctx.enter_context(tc.tile_pool(name="keep", bufs=1))
-        work = ctx.enter_context(tc.tile_pool(name="work", bufs=3))
-        flip_banks = ctx.enter_context(tc.psum_pool(name="flip_banks", bufs=5))
-        ov_banks = ctx.enter_context(tc.psum_pool(name="ov_banks", bufs=1))
-        mean_banks = ctx.enter_context(tc.psum_pool(name="mean_banks", bufs=1))
+        work = ctx.enter_context(tc.tile_pool(name="work", bufs=ROW_TILES))
+        banks = ctx.enter_context(tc.psum_pool(name="banks", bufs=7))
         last_banks = ctx.enter_context(tc.psum_pool(name="last_banks", bufs=1))
         ctx.enter_context(tc.manual_schedule())
 
@@ -56,13 +55,16 @@ def tile_quantumkernelpca_s_kernel(tc, x, x_ref, mean_, components_, out):
         ident_f32 = keep.tile([P, P], F32)
         make_identity(nc, ident_f32[:])
 
-        mean_bank = mean_banks.tile([P, MEAN_WORDS, P], F32)
-        for j in range(MEAN_WORDS):
-            nc.tensor.transpose(
-                mean_bank[:, j, :],
-                mean_sb[:].bitcast(F32)[:, j : j + 1].to_broadcast([P, P]),
-                ident_f32[:],
-            )
+        mean_bank = banks.tile([P, MEAN_WORDS, P], F32, name="bank")
+        mean_bank_2 = banks.tile([P, MEAN_WORDS, P], F32, name="bank")
+        for mb in (mean_bank, mean_bank_2):
+            for j in range(MEAN_WORDS):
+                nc.tensor.transpose(
+                    mb[:, j, :],
+                    mean_sb[:].bitcast(F32)[:, j : j + 1].to_broadcast([P, P]),
+                    ident_f32[:],
+                )
+        mean_gp = keep.tile([P, F], BF16)
         mean_bc = mean_bank[:].bitcast(BF16).rearrange("q j (p e) -> q p j e", e=2)
 
         def by_mean_words(rows):
@@ -73,6 +75,10 @@ def tile_quantumkernelpca_s_kernel(tc, x, x_ref, mean_, components_, out):
         one_root = keep.tile([P, 1], F32)
         nc.scalar.activation(out=one_root[:], in_=one[:], func=ACT.Sqrt)
 
+        nc.scalar.copy(
+            out=mean_gp[:].bitcast(F32).rearrange("q (p j) -> q p j", j=MEAN_WORDS),
+            in_=mean_bank_2[:].rearrange("q j p -> q p j"),
+        )
         centred = keep.tile([P, ROW_TILES, F], F32)
         norm_sq = keep.tile([P, ROW_TILES], F32)
         norm = keep.tile([P, ROW_TILES], F32)
@@ -97,7 +103,7 @@ def tile_quantumkernelpca_s_kernel(tc, x, x_ref, mean_, components_, out):
 
         def flip_components():
             words = comp_sb[:].bitcast(F32).rearrange("c (g p u) -> c g u p", g=R_PASSES, u=2)
-            comp_flip = flip_banks.tile([P, R_PASSES, 2, C], F32, name="bank")
+            comp_flip = banks.tile([P, R_PASSES, 2, C], F32, name="bank")
             flipped["components"] = comp_flip
             for g in range(R_PASSES):
                 for u in range(2):
@@ -124,13 +130,20 @@ def tile_quantumkernelpca_s_kernel(tc, x, x_ref, mean_, components_, out):
             g, t = divmod(j - 1, PACK)
             return ref_sb[:, g, t, :]
 
+        def subtract(j):
+            if j in GPSIMD_TILES:
+                nc.gpsimd.tensor_tensor(
+                    out=centred[:, j, :], in0=rows_of(j), in1=mean_gp[:], op=ALU.subtract
+                )
+            else:
+                nc.vector.tensor_tensor(
+                    out=by_mean_words(centred[:, j, :]),
+                    in0=by_mean_words(rows_of(j)),
+                    in1=mean_bc,
+                    op=ALU.subtract,
+                )
+
         def measure(j):
-            nc.vector.tensor_tensor(
-                out=by_mean_words(centred[:, j, :]),
-                in0=by_mean_words(rows_of(j)),
-                in1=mean_bc,
-                op=ALU.subtract,
-            )
             squares = work.tile([P, F], BF16, name="squares")
             nc.scalar.activation(
                 out=squares[:], in_=centred[:, j, :], func=ACT.Square,
@@ -150,7 +163,7 @@ def tile_quantumkernelpca_s_kernel(tc, x, x_ref, mean_, components_, out):
                 out=state[:], in0=centred[:, j, :], scalar1=inv_norm[:, j : j + 1]
             )
             words = state[:].bitcast(F32).rearrange("r (c u p) -> r c u p", c=F_PASSES, u=2)
-            bank = flip_banks.tile([P, F_PASSES, 2, P], F32, name="bank")
+            bank = banks.tile([P, F_PASSES, 2, P], F32, name="bank")
             flipped[j] = bank
             for c in range(F_PASSES):
                 for u in range(2):
@@ -163,7 +176,7 @@ def tile_quantumkernelpca_s_kernel(tc, x, x_ref, mean_, components_, out):
                 "p (c r u) -> p c r u", c=F_PASSES, u=2
             )
             by_words = flipped[j][:].rearrange("p c u r -> p c r u")
-            if j == 0 or j == ROW_TILES - 1:
+            if j == ROW_TILES - 1:
                 nc.vector.tensor_copy(out=pairs, in_=by_words)
             else:
                 nc.scalar.copy(out=pairs, in_=by_words)
@@ -176,7 +189,7 @@ def tile_quantumkernelpca_s_kernel(tc, x, x_ref, mean_, components_, out):
             )
 
         def overlaps(g):
-            overlap[g] = ov_banks.tile([P, PACK, N], F32, name="ov")
+            overlap[g] = banks.tile([P, PACK, N], F32, name="bank")
             for t in range(PACK):
                 j = 1 + g * PACK + t
                 for c in range(F_PASSES):
@@ -213,30 +226,32 @@ def tile_quantumkernelpca_s_kernel(tc, x, x_ref, mean_, components_, out):
                 stop=(g == R_PASSES - 1),
             )
 
+        for j in range(ROW_TILES):
+            subtract(j)
         for lo, hi in GROUPS:
             for j in range(lo, hi):
                 measure(j)
             roots(lo, hi)
 
-        for k in range(ROW_TILES + 5):
+        for k in range(ROW_TILES):
             for lo, hi in GROUPS:
                 if k == lo:
                     invert(lo, hi)
-            if k < ROW_TILES:
-                normalise_and_flip(k)
-            if 0 <= k - 2 < ROW_TILES:
-                regroup(k - 2)
-            if 0 <= k - 3 < ROW_TILES:
-                quantise_state(k - 3)
-            if pass_ending_at(k - 4) is not None:
-                overlaps(pass_ending_at(k - 4))
-            if k == ROW_TILES - 1:
-                flip_components()
-            if k - 3 == ROW_TILES - 1:
-                regroup_components()
-                quantise_components()
-            if pass_ending_at(k - 5) is not None:
-                square_overlaps(pass_ending_at(k - 5))
+            normalise_and_flip(k)
+        flip_components()
+        for j in range(ROW_TILES):
+            if j == 5:
+                regroup(ROW_TILES - 1)
+            if j < ROW_TILES - 1:
+                regroup(j)
+            quantise_state(j)
+            if j == PACK:
+                overlaps(0)
+        regroup_components()
+        square_overlaps(0)
+        overlaps(1)
+        quantise_components()
+        square_overlaps(1)
         for g in range(R_PASSES):
             project(g)
 

@@ -44,7 +44,7 @@ def tile_quantumkernelpca_s_kernel(tc, x, x_ref, mean_, components_, out):
         x_sb = keep.tile([P, F], BF16)
         mean_sb = keep.tile([P, F // P], BF16)
         ref_sb = keep.tile([P, R_PASSES, PACK, F], BF16)
-        nc.scalar.dma_start(out=mean_sb[:], in_=mean_.rearrange("(p k) -> p k", p=P))
+        nc.sync.dma_start(out=mean_sb[:], in_=mean_.rearrange("(p k) -> p k", p=P))
         nc.sync.dma_start(out=x_sb[:], in_=x)
         ref_rows = x_ref.rearrange("(g p t) f -> g p t f", g=R_PASSES, p=P, t=PACK)
         for g in range(R_PASSES):
@@ -153,8 +153,10 @@ def tile_quantumkernelpca_s_kernel(tc, x, x_ref, mean_, components_, out):
         def roots(lo, hi):
             nc.scalar.activation(out=norm[:, lo:hi], in_=norm_sq[:, lo:hi], func=ACT.Sqrt)
 
-        def invert(lo, hi):
+        def add_eps(lo, hi):
             nc.vector.tensor_scalar_add(out=norm_eps[:, lo:hi], in0=norm[:, lo:hi], scalar1=EPS)
+
+        def invert(lo, hi):
             nc.vector.reciprocal(out=inv_norm[:, lo:hi], in_=norm_eps[:, lo:hi])
 
         def normalise_and_flip(j):
@@ -176,7 +178,7 @@ def tile_quantumkernelpca_s_kernel(tc, x, x_ref, mean_, components_, out):
                 "p (c r u) -> p c r u", c=F_PASSES, u=2
             )
             by_words = flipped[j][:].rearrange("p c u r -> p c r u")
-            if j == ROW_TILES - 1:
+            if j == 0:
                 nc.vector.tensor_copy(out=pairs, in_=by_words)
             else:
                 nc.scalar.copy(out=pairs, in_=by_words)
@@ -226,24 +228,32 @@ def tile_quantumkernelpca_s_kernel(tc, x, x_ref, mean_, components_, out):
                 stop=(g == R_PASSES - 1),
             )
 
-        for j in range(ROW_TILES):
+        first, last = GROUPS[0], ROW_TILES - 1
+        for j in range(last):
             subtract(j)
-        for lo, hi in GROUPS:
-            for j in range(lo, hi):
+        for group in GROUPS:
+            for j in range(*group):
                 measure(j)
-            roots(lo, hi)
+            roots(*group)
+            if group == first:
+                add_eps(*group)
+                subtract(last)
+                invert(*group)
 
         for k in range(ROW_TILES):
-            for lo, hi in GROUPS:
-                if k == lo:
-                    invert(lo, hi)
+            following = [group for group in GROUPS if group[0] == k + 1]
+            if k == 6:
+                regroup(0)
+            for group in following:
+                add_eps(*group)
             normalise_and_flip(k)
+            for group in following:
+                invert(*group)
+            if k == 6:
+                quantise_state(0)
         flip_components()
-        for j in range(ROW_TILES):
-            if j == 5:
-                regroup(ROW_TILES - 1)
-            if j < ROW_TILES - 1:
-                regroup(j)
+        for j in range(1, ROW_TILES):
+            regroup(j)
             quantise_state(j)
             if j == PACK:
                 overlaps(0)

@@ -17,7 +17,8 @@ K_PASS = P * PACK
 N, NR, F, C = 128, 1024, 1024, 128
 EPS = 1e-8
 MEAN_WORDS = F // P // 2
-GPSIMD_TILES = (3, 6)
+HALF = F // 2
+GPSIMD_FEATURES = {1: HALF, 3: F, 5: F, 8: HALF}
 F_PASSES = F // K_PASS
 R_PASSES = NR // K_PASS
 ROW_TILES = 1 + NR // P
@@ -56,14 +57,12 @@ def tile_quantumkernelpca_s_kernel(tc, x, x_ref, mean_, components_, out):
         make_identity(nc, ident_f32[:])
 
         mean_bank = banks.tile([P, MEAN_WORDS, P], F32, name="bank")
-        mean_bank_2 = banks.tile([P, MEAN_WORDS, P], F32, name="bank")
-        for mb in (mean_bank, mean_bank_2):
-            for j in range(MEAN_WORDS):
-                nc.tensor.transpose(
-                    mb[:, j, :],
-                    mean_sb[:].bitcast(F32)[:, j : j + 1].to_broadcast([P, P]),
-                    ident_f32[:],
-                )
+        for j in range(MEAN_WORDS):
+            nc.tensor.transpose(
+                mean_bank[:, j, :],
+                mean_sb[:].bitcast(F32)[:, j : j + 1].to_broadcast([P, P]),
+                ident_f32[:],
+            )
         mean_gp = keep.tile([P, F], BF16)
         mean_bc = mean_bank[:].bitcast(BF16).rearrange("q j (p e) -> q p j e", e=2)
 
@@ -75,9 +74,9 @@ def tile_quantumkernelpca_s_kernel(tc, x, x_ref, mean_, components_, out):
         one_root = keep.tile([P, 1], F32)
         nc.scalar.activation(out=one_root[:], in_=one[:], func=ACT.Sqrt)
 
-        nc.scalar.copy(
+        nc.vector.tensor_copy(
             out=mean_gp[:].bitcast(F32).rearrange("q (p j) -> q p j", j=MEAN_WORDS),
-            in_=mean_bank_2[:].rearrange("q j p -> q p j"),
+            in_=mean_bank[:].rearrange("q j p -> q p j"),
         )
         centred = keep.tile([P, ROW_TILES, F], F32)
         norm_sq = keep.tile([P, ROW_TILES], F32)
@@ -130,24 +129,27 @@ def tile_quantumkernelpca_s_kernel(tc, x, x_ref, mean_, components_, out):
             g, t = divmod(j - 1, PACK)
             return ref_sb[:, g, t, :]
 
-        def subtract(j):
-            if j in GPSIMD_TILES:
+        def subtract(j, lo=0, hi=F):
+            cut = max(lo, GPSIMD_FEATURES.get(j, 0))
+            if lo < cut:
                 nc.gpsimd.tensor_tensor(
-                    out=centred[:, j, :], in0=rows_of(j), in1=mean_gp[:], op=ALU.subtract
+                    out=centred[:, j, lo:cut], in0=rows_of(j)[:, lo:cut], in1=mean_gp[:, lo:cut],
+                    op=ALU.subtract,
                 )
-            else:
+            if cut < hi:
+                run = F // P
                 nc.vector.tensor_tensor(
-                    out=by_mean_words(centred[:, j, :]),
-                    in0=by_mean_words(rows_of(j)),
-                    in1=mean_bc,
+                    out=by_mean_words(centred[:, j, cut:hi]),
+                    in0=by_mean_words(rows_of(j)[:, cut:hi]),
+                    in1=mean_bc[:, cut // run : hi // run, :, :],
                     op=ALU.subtract,
                 )
 
-        def measure(j):
+        def measure(j, lo=0, hi=F, total=None):
             squares = work.tile([P, F], BF16, name="squares")
             nc.scalar.activation(
-                out=squares[:], in_=centred[:, j, :], func=ACT.Square,
-                accum_out=norm_sq[:, j : j + 1],
+                out=squares[:, lo:hi], in_=centred[:, j, lo:hi], func=ACT.Square,
+                accum_out=norm_sq[:, j : j + 1] if total is None else total,
             )
 
         def roots(lo, hi):
@@ -228,30 +230,37 @@ def tile_quantumkernelpca_s_kernel(tc, x, x_ref, mean_, components_, out):
                 stop=(g == R_PASSES - 1),
             )
 
-        first, last = GROUPS[0], ROW_TILES - 1
-        for j in range(last):
+        flip_components()
+        half_sums = keep.tile([P, 2], F32)
+        for i in range(2):
+            subtract(0, i * HALF, (i + 1) * HALF)
+            measure(0, i * HALF, (i + 1) * HALF, half_sums[:, i : i + 1])
+        for j in range(1, ROW_TILES - 1):
+            if j == 6:
+                nc.vector.tensor_add(
+                    out=norm_sq[:, 0:1], in0=half_sums[:, 0:1], in1=half_sums[:, 1:2]
+                )
             subtract(j)
         for group in GROUPS:
-            for j in range(*group):
+            for j in range(max(1, group[0]), group[1]):
                 measure(j)
             roots(*group)
-            if group == first:
+            if group == GROUPS[0]:
                 add_eps(*group)
-                subtract(last)
+                subtract(ROW_TILES - 1)
                 invert(*group)
 
         for k in range(ROW_TILES):
             following = [group for group in GROUPS if group[0] == k + 1]
-            if k == 6:
+            if k == 3:
                 regroup(0)
+            if k == 6:
+                quantise_state(0)
             for group in following:
                 add_eps(*group)
             normalise_and_flip(k)
             for group in following:
                 invert(*group)
-            if k == 6:
-                quantise_state(0)
-        flip_components()
         for j in range(1, ROW_TILES):
             regroup(j)
             quantise_state(j)

@@ -100,6 +100,12 @@ def tile_quantumkernelpca_s_kernel(tc, x, x_ref, mean_, components_, out):
 
         comp_grouped = keep.tile([P, R_PASSES, C * PACK], BF16, align_bytes=64)
 
+        def warm_up(times):
+            for i in range(times):
+                nc.tensor.matmul(
+                    out_acc[:], lhsT=ident_f32[:], rhs=ident_f32[:], start=True, stop=True
+                )
+
         def flip_components():
             words = comp_sb[:].bitcast(F32).rearrange("c (g p u) -> c g u p", g=R_PASSES, u=2)
             comp_flip = banks.tile([P, R_PASSES, 2, C], F32, name="bank")
@@ -231,6 +237,7 @@ def tile_quantumkernelpca_s_kernel(tc, x, x_ref, mean_, components_, out):
             )
 
         flip_components()
+        warm_up(3)
         half_sums = keep.tile([P, 2], F32)
         for i in range(2):
             subtract(0, i * HALF, (i + 1) * HALF)
@@ -261,6 +268,8 @@ def tile_quantumkernelpca_s_kernel(tc, x, x_ref, mean_, components_, out):
             normalise_and_flip(k)
             for group in following:
                 invert(*group)
+            if k % 2 == 1:
+                warm_up(1)
         for j in range(1, ROW_TILES):
             regroup(j)
             quantise_state(j)

@@ -18,7 +18,7 @@ N, NR, F, C = 128, 1024, 1024, 128
 EPS = 1e-8
 MEAN_WORDS = F // P // 2
 HALF = F // 2
-GPSIMD_FEATURES = {1: HALF, 3: F, 5: F, 8: HALF}
+GPSIMD_FEATURES = {1: HALF, 3: F, 5: F, 8: HALF // 2}
 F_PASSES = F // K_PASS
 R_PASSES = NR // K_PASS
 ROW_TILES = 1 + NR // P

from contextlib import ExitStack

import concourse.mybir as mybir
from concourse.masks import make_identity

BF16 = mybir.dt.bfloat16
F32 = mybir.dt.float32
U32 = mybir.dt.uint32
U8 = mybir.dt.uint8
FP8X4 = mybir.dt.float8_e4m3fn_x4
ACT = mybir.ActivationFunctionType
ALU = mybir.AluOpType

P = 128
PACK = 4
K_PASS = P * PACK
N, NR, F, C = 128, 1024, 1024, 128
EPS = 1e-8
MEAN_WORDS = F // P // 2
HALF = F // 2
GPSIMD_FEATURES = {1: HALF, 3: F, 5: F, 8: HALF // 2}
F_PASSES = F // K_PASS
R_PASSES = NR // K_PASS
ROW_TILES = 1 + NR // P
GROUPS = ((0, 4), (4, 7), (7, 9))
FLOPS = 2 * N * NR * F + 2 * N * C * NR


def pass_ending_at(j):
    if j >= 1 and j < ROW_TILES and (j - 1) % PACK == PACK - 1:
        return (j - 1) // PACK
    return None


def tile_quantumkernelpca_s_kernel(tc, x, x_ref, mean_, components_, out):
    nc = tc.nc
    with ExitStack() as ctx:
        keep = ctx.enter_context(tc.tile_pool(name="keep", bufs=1))
        work = ctx.enter_context(tc.tile_pool(name="work", bufs=ROW_TILES))
        banks = ctx.enter_context(tc.psum_pool(name="banks", bufs=7))
        last_banks = ctx.enter_context(tc.psum_pool(name="last_banks", bufs=1))
        ctx.enter_context(tc.manual_schedule())

        comp_sb = keep.tile([P, NR], BF16)
        x_sb = keep.tile([P, F], BF16)
        mean_sb = keep.tile([P, F // P], BF16)
        ref_sb = keep.tile([P, R_PASSES, PACK, F], BF16)
        nc.sync.dma_start(out=mean_sb[:], in_=mean_.rearrange("(p k) -> p k", p=P))
        nc.sync.dma_start(out=x_sb[:], in_=x)
        ref_rows = x_ref.rearrange("(g p t) f -> g p t f", g=R_PASSES, p=P, t=PACK)
        for g in range(R_PASSES):
            for t in range(0, PACK, 2):
                nc.sync.dma_start(out=ref_sb[:, g, t : t + 2, :], in_=ref_rows[g, :, t : t + 2, :])
        nc.sync.dma_start(out=comp_sb[:], in_=components_)

        ident_f32 = keep.tile([P, P], F32)
        make_identity(nc, ident_f32[:])

        mean_bank = banks.tile([P, MEAN_WORDS, P], F32, name="bank")
        for j in range(MEAN_WORDS):
            nc.tensor.transpose(
                mean_bank[:, j, :],
                mean_sb[:].bitcast(F32)[:, j : j + 1].to_broadcast([P, P]),
                ident_f32[:],
            )
        mean_gp = keep.tile([P, F], BF16)
        mean_bc = mean_bank[:].bitcast(BF16).rearrange("q j (p e) -> q p j e", e=2)

        def by_mean_words(rows):
            return rows.rearrange("q (p j e) -> q p j e", j=MEAN_WORDS, e=2)

        one = keep.tile([P, 1], F32)
        nc.vector.memset(one[:], 1.0)
        one_root = keep.tile([P, 1], F32)
        nc.scalar.activation(out=one_root[:], in_=one[:], func=ACT.Sqrt)

        nc.vector.tensor_copy(
            out=mean_gp[:].bitcast(F32).rearrange("q (p j) -> q p j", j=MEAN_WORDS),
            in_=mean_bank[:].rearrange("q j p -> q p j"),
        )
        centred = keep.tile([P, ROW_TILES, F], F32)
        norm_sq = keep.tile([P, ROW_TILES], F32)
        norm = keep.tile([P, ROW_TILES], F32)
        norm_eps = keep.tile([P, ROW_TILES], F32)
        inv_norm = keep.tile([P, ROW_TILES], F32)

        state_codes = keep.tile([P, ROW_TILES, F_PASSES, P], U32, align_bytes=64)
        state_scales = keep.tile([P, ROW_TILES, F_PASSES, P], U8, align_bytes=64)
        comp_codes = keep.tile([P, R_PASSES, C], U32, align_bytes=64)
        comp_scales = keep.tile([P, R_PASSES, C], U8, align_bytes=64)
        kern_codes = keep.tile([P, R_PASSES, N], U32, align_bytes=64)
        kern_scales = keep.tile([P, R_PASSES, N], U8, align_bytes=64)

        out_acc = last_banks.tile([N, C], F32)

        flipped = {}
        packed = {}
        overlap = {}
        kernel = {}

        comp_grouped = keep.tile([P, R_PASSES, C * PACK], BF16, align_bytes=64)

        def warm_up(times):
            for i in range(times):
                nc.tensor.matmul(
                    out_acc[:], lhsT=ident_f32[:], rhs=ident_f32[:], start=True, stop=True
                )

        def flip_components():
            words = comp_sb[:].bitcast(F32).rearrange("c (g p u) -> c g u p", g=R_PASSES, u=2)
            comp_flip = banks.tile([P, R_PASSES, 2, C], F32, name="bank")
            flipped["components"] = comp_flip
            for g in range(R_PASSES):
                for u in range(2):
                    nc.tensor.transpose(comp_flip[:, g, u, :], words[:, g, u, :], ident_f32[:])

        def regroup_components():
            nc.scalar.copy(
                out=comp_grouped[:].rearrange("p g w -> p (g w)").bitcast(F32).rearrange(
                    "p (g c u) -> p g c u", g=R_PASSES, u=2
                ),
                in_=flipped["components"][:].rearrange("p g u c -> p g c u"),
            )

        def quantise_components():
            nc.vector.quantize_mx(
                out=comp_codes[:].rearrange("p g c -> p (g c)").bitcast(FP8X4),
                scales=comp_scales[:].rearrange("p g c -> p (g c)"),
                in_=comp_grouped[:].rearrange("p g w -> p (g w)"),
            )

        def rows_of(j):
            if j == 0:
                return x_sb[:]
            g, t = divmod(j - 1, PACK)
            return ref_sb[:, g, t, :]

        def subtract(j, lo=0, hi=F):
            cut = max(lo, GPSIMD_FEATURES.get(j, 0))
            if lo < cut:
                nc.gpsimd.tensor_tensor(
                    out=centred[:, j, lo:cut], in0=rows_of(j)[:, lo:cut], in1=mean_gp[:, lo:cut],
                    op=ALU.subtract,
                )
            if cut < hi:
                run = F // P
                nc.vector.tensor_tensor(
                    out=by_mean_words(centred[:, j, cut:hi]),
                    in0=by_mean_words(rows_of(j)[:, cut:hi]),
                    in1=mean_bc[:, cut // run : hi // run, :, :],
                    op=ALU.subtract,
                )

        def measure(j, lo=0, hi=F, total=None):
            squares = work.tile([P, F], BF16, name="squares")
            nc.scalar.activation(
                out=squares[:, lo:hi], in_=centred[:, j, lo:hi], func=ACT.Square,
                accum_out=norm_sq[:, j : j + 1] if total is None else total,
            )

        def roots(lo, hi):
            nc.scalar.activation(out=norm[:, lo:hi], in_=norm_sq[:, lo:hi], func=ACT.Sqrt)

        def add_eps(lo, hi):
            nc.vector.tensor_scalar_add(out=norm_eps[:, lo:hi], in0=norm[:, lo:hi], scalar1=EPS)

        def invert(lo, hi):
            nc.vector.reciprocal(out=inv_norm[:, lo:hi], in_=norm_eps[:, lo:hi])

        def normalise_and_flip(j):
            state = work.tile([P, F], BF16, name="state")
            nc.vector.tensor_scalar_mul(
                out=state[:], in0=centred[:, j, :], scalar1=inv_norm[:, j : j + 1]
            )
            words = state[:].bitcast(F32).rearrange("r (c u p) -> r c u p", c=F_PASSES, u=2)
            bank = banks.tile([P, F_PASSES, 2, P], F32, name="bank")
            flipped[j] = bank
            for c in range(F_PASSES):
                for u in range(2):
                    nc.tensor.transpose(bank[:, c, u, :], words[:, c, u, :], ident_f32[:])

        def regroup(j):
            grouped = work.tile([P, F_PASSES, P, PACK], BF16, name="grouped", align_bytes=64)
            packed[j] = grouped
            pairs = grouped[:].rearrange("p c r t -> p (c r t)").bitcast(F32).rearrange(
                "p (c r u) -> p c r u", c=F_PASSES, u=2
            )
            by_words = flipped[j][:].rearrange("p c u r -> p c r u")
            if j == 0:
                nc.vector.tensor_copy(out=pairs, in_=by_words)
            else:
                nc.scalar.copy(out=pairs, in_=by_words)

        def quantise_state(j):
            nc.vector.quantize_mx(
                out=state_codes[:, j, :, :].rearrange("p c r -> p (c r)").bitcast(FP8X4),
                scales=state_scales[:, j, :, :].rearrange("p c r -> p (c r)"),
                in_=packed[j][:].rearrange("p c r t -> p (c r t)"),
            )

        def overlaps(g):
            overlap[g] = banks.tile([P, PACK, N], F32, name="bank")
            for t in range(PACK):
                j = 1 + g * PACK + t
                for c in range(F_PASSES):
                    nc.tensor.matmul_mx(
                        out=overlap[g][:, t, :],
                        lhsT=state_codes[:, j, c, :].bitcast(FP8X4),
                        lhsT_scale=state_scales[:, j, c, :],
                        rhs=state_codes[:, 0, c, :].bitcast(FP8X4),
                        rhs_scale=state_scales[:, 0, c, :],
                        start=(c == 0),
                        stop=(c == F_PASSES - 1),
                    )

        def square_overlaps(g):
            kern_grouped = work.tile([P, N, PACK], BF16, name="kern_grouped", align_bytes=64)
            kernel[g] = kern_grouped
            nc.scalar.activation(
                out=kern_grouped[:], in_=overlap[g][:].rearrange("p t n -> p n t"), func=ACT.Square
            )

        def project(g):
            nc.vector.quantize_mx(
                out=kern_codes[:, g, :].bitcast(FP8X4),
                scales=kern_scales[:, g, :],
                in_=kernel[g][:].rearrange("p n t -> p (n t)"),
            )
            nc.tensor.matmul_mx(
                out=out_acc[:],
                lhsT=kern_codes[:, g, :].bitcast(FP8X4),
                lhsT_scale=kern_scales[:, g, :],
                rhs=comp_codes[:, g, :].bitcast(FP8X4),
                rhs_scale=comp_scales[:, g, :],
                start=(g == 0),
                stop=(g == R_PASSES - 1),
            )

        flip_components()
        warm_up(3)
        half_sums = keep.tile([P, 2], F32)
        for i in range(2):
            subtract(0, i * HALF, (i + 1) * HALF)
            measure(0, i * HALF, (i + 1) * HALF, half_sums[:, i : i + 1])
        for j in range(1, ROW_TILES - 1):
            if j == 6:
                nc.vector.tensor_add(
                    out=norm_sq[:, 0:1], in0=half_sums[:, 0:1], in1=half_sums[:, 1:2]
                )
            subtract(j)
        for group in GROUPS:
            for j in range(max(1, group[0]), group[1]):
                measure(j)
            roots(*group)
            if group == GROUPS[0]:
                add_eps(*group)
                subtract(ROW_TILES - 1)
                invert(*group)

        for k in range(ROW_TILES):
            following = [group for group in GROUPS if group[0] == k + 1]
            if k == 3:
                regroup(0)
            if k == 6:
                quantise_state(0)
            for group in following:
                add_eps(*group)
            normalise_and_flip(k)
            for group in following:
                invert(*group)
            if k % 2 == 1:
                warm_up(1)
        for j in range(1, ROW_TILES):
            regroup(j)
            quantise_state(j)
            if j == PACK:
                overlaps(0)
        regroup_components()
        square_overlaps(0)
        overlaps(1)
        quantise_components()
        square_overlaps(1)
        for g in range(R_PASSES):
            project(g)

        result = keep.tile([N, C], F32)
        nc.vector.tensor_copy(out=result[:], in_=out_acc[:])
        nc.sync.dma_start(out=out, in_=result[:])
